import numpy as np
import ml_dtypes

BF16 = ml_dtypes.bfloat16


def bf(x):
    return np.asarray(x, np.float32).astype(BF16)


def f32(x):
    return np.asarray(x, np.float32)


def f64(x):
    return np.asarray(x).astype(np.float64)


def striped(idx):
    return np.tile(idx.reshape(-1, 16).T, (8, 1))


D, T, S, N = 128, 1024, 1024, 1024
SCALE = 1.0 / np.sqrt(D)
MASK_STD = 1.5
V_STD = 2.0


def setup_inputs():
    return {"mask": f32(MASK_STD * np.random.standard_normal((T, S))), "q": bf(np.random.standard_normal((D, N))), "kc": bf(np.random.standard_normal((D, T))), "vc": bf(V_STD * np.random.standard_normal((T, D))), "offs": striped(np.random.permutation(S)[:N])}


def reference(mask, q, kc, vc, offs):
    idx = offs[:16].T.reshape(-1)
    w = SCALE * (f64(kc).T @ f64(q)) + f64(mask)[:, idx]
    e = np.exp(w)
    p = e / e.sum(axis=0, keepdims=True)
    return f64(vc).T @ p

@@ -1,0 +1,113 @@
+import math
+
+import concourse.mybir as mybir
+from concourse.masks import make_identity
+
+F32 = mybir.dt.float32
+BF16 = mybir.dt.bfloat16
+U16 = mybir.dt.uint16
+ADD = mybir.AluOpType.add
+COPY = mybir.ActivationFunctionType.Copy
+EXP = mybir.ActivationFunctionType.Exp
+
+P = 128
+D, T, S, N = 128, 1024, 1024, 1024
+SCALE = 1.0 / math.sqrt(D)
+KEY_BLOCKS = T // P
+PIECE = 512
+PIECES = N // PIECE
+SUBS = PIECE // P
+STEPS = PIECES * KEY_BLOCKS
+VC_PITCH = 144
+AHEAD = 2
+FLOPS = 4 * D * T * N
+
+
+def tile_sdpasimple_kernel(tc, mask, q, kc, vc, offs, out):
+    nc = tc.nc
+    with (
+        tc.tile_pool(name="held", bufs=1) as held,
+        tc.tile_pool(name="work", bufs=3) as work,
+        tc.psum_pool(name="score_banks", bufs=3) as score_banks,
+        tc.psum_pool(name="product_banks", bufs=1) as product_banks,
+    ):
+        offsets = held.tile([P, N // 16], U16, name="offsets")
+        nc.sync.dma_start(offsets[:], offs)
+        kc_sb = held.tile([D, T], BF16, name="kc_sb")
+        nc.scalar.dma_start(kc_sb[:], kc)
+        q_sb = held.tile([D, N], BF16, name="q_sb")
+        nc.scalar.dma_start(q_sb[:], q)
+        mask_sb = []
+        for b in range(KEY_BLOCKS):
+            window = held.tile([P, S], F32, name=f"mask{b}")
+            nc.sync.dma_start(window[:], mask[b * P : (b + 1) * P, :])
+            mask_sb.append(window)
+        vc_ones = held.tile([P, KEY_BLOCKS, VC_PITCH], BF16, name="vc_ones")
+        nc.gpsimd.memset(vc_ones[:, :, D:VC_PITCH], 1.0)
+        nc.gpsimd.dma_start(vc_ones[:, :, 0:D], vc.rearrange("(b p) d -> p b d", p=P))
+        identity = held.tile([P, P], F32, name="identity")
+        make_identity(nc, identity[:])
+
+        scaled = {}
+        products = {}
+
+        def scores(step):
+            piece, b = divmod(step, KEY_BLOCKS)
+            score_ps = score_banks.tile([P, PIECE], F32, name="score_ps")
+            nc.tensor.matmul(
+                score_ps[:],
+                kc_sb[:, b * P : (b + 1) * P],
+                q_sb[:, piece * PIECE : (piece + 1) * PIECE],
+                start=True,
+                stop=True,
+            )
+            scaled_sb = work.tile([P, PIECE], F32, name="scaled_sb")
+            nc.scalar.activation(scaled_sb[:], score_ps[:], COPY, scale=SCALE)
+            scaled[step] = scaled_sb
+
+        def weights(step):
+            piece, b = divmod(step, KEY_BLOCKS)
+            cols = PIECE // 16
+            w_sb = work.tile([P, PIECE], F32, name="w_sb")
+            nc.vector.tensor_tensor(
+                w_sb[:],
+                mask_sb[b][:].indirect(offsets[:, piece * cols : (piece + 1) * cols]),
+                scaled.pop(step)[:],
+                ADD,
+            )
+            e_sb = work.tile([P, PIECE], BF16, name="e_sb")
+            nc.scalar.activation(e_sb[:], w_sb[:], EXP)
+            if b == 0:
+                products[piece] = [
+                    product_banks.tile([P, D + 1], F32, name=f"product{c}") for c in range(SUBS)
+                ]
+            for c in range(SUBS):
+                nc.tensor.matmul(
+                    products[piece][c][:],
+                    e_sb[:, c * P : (c + 1) * P],
+                    vc_ones[:, b, 0 : D + 1],
+                    start=(b == 0),
+                    stop=(b == KEY_BLOCKS - 1),
+                )
+
+        def finish(piece):
+            out_ps = product_banks.tile([D, PIECE], F32, name="out_ps")
+            for c, product in enumerate(products.pop(piece)):
+                inverse = work.tile([P, 1], F32, name="inverse")
+                nc.vector.reciprocal(inverse[:], product[:, D : D + 1])
+                normal = work.tile([P, D], F32, name="normal")
+                nc.scalar.activation(normal[:], product[:, 0:D], COPY, scale=inverse[:])
+                nc.tensor.transpose(out_ps[:, c * P : (c + 1) * P], normal[:], identity[:])
+            out_sb = work.tile([D, PIECE], F32, name="out_sb")
+            nc.vector.tensor_copy(out_sb[:], out_ps[:])
+            nc.sync.dma_start(out[:, piece * PIECE : (piece + 1) * PIECE], out_sb[:])
+
+        for step in range(AHEAD):
+            scores(step)
+        for step in range(STEPS):
+            if step + AHEAD < STEPS:
+                scores(step + AHEAD)
+            weights(step)
+            if step >= KEY_BLOCKS and step % KEY_BLOCKS == AHEAD:
+                finish(step // KEY_BLOCKS - 1)
+        finish(PIECES - 1)

@@ -27,24 +27,26 @@ def tile_sdpasimple_kernel(tc, mask, q, kc, vc, offs, out):
     nc = tc.nc
     with (
         tc.tile_pool(name="held", bufs=1) as held,
-        tc.tile_pool(name="work", bufs=3) as work,
+        tc.tile_pool(name="work", bufs=4) as work,
         tc.psum_pool(name="score_banks", bufs=3) as score_banks,
         tc.psum_pool(name="product_banks", bufs=1) as product_banks,
     ):
         offsets = held.tile([P, N // 16], U16, name="offsets")
         nc.sync.dma_start(offsets[:], offs)
-        kc_sb = held.tile([D, T], BF16, name="kc_sb")
-        nc.scalar.dma_start(kc_sb[:], kc)
-        q_sb = held.tile([D, N], BF16, name="q_sb")
-        nc.scalar.dma_start(q_sb[:], q)
         mask_sb = []
         for b in range(KEY_BLOCKS):
             window = held.tile([P, S], F32, name=f"mask{b}")
             nc.sync.dma_start(window[:], mask[b * P : (b + 1) * P, :])
             mask_sb.append(window)
+        kc_sb = held.tile([D, T], BF16, name="kc_sb")
+        q_sb = held.tile([D, N], BF16, name="q_sb")
         vc_ones = held.tile([P, KEY_BLOCKS, VC_PITCH], BF16, name="vc_ones")
         nc.gpsimd.memset(vc_ones[:, :, D:VC_PITCH], 1.0)
-        nc.gpsimd.dma_start(vc_ones[:, :, 0:D], vc.rearrange("(b p) d -> p b d", p=P))
+        nc.scalar.dma_start(kc_sb[:, 0 : T // 2], kc[:, 0 : T // 2])
+        nc.scalar.dma_start(q_sb[:, 0:PIECE], q[:, 0:PIECE])
+        nc.scalar.dma_start(vc_ones[:, :, 0:D], vc.rearrange("(b p) d -> p b d", p=P))
+        nc.scalar.dma_start(kc_sb[:, T // 2 : T], kc[:, T // 2 : T])
+        nc.scalar.dma_start(q_sb[:, PIECE:N], q[:, PIECE:N])
         identity = held.tile([P, P], F32, name="identity")
         make_identity(nc, identity[:])
 

@@ -14,9 +14,10 @@ P = 128
 D, T, S, N = 128, 1024, 1024, 1024
 SCALE = 1.0 / math.sqrt(D)
 KEY_BLOCKS = T // P
-PIECE = 512
-PIECES = N // PIECE
-SUBS = PIECE // P
+BANK = 512
+WIDTHS = (BANK, N - BANK - P, P)
+STARTS = (0, BANK, N - P)
+PIECES = len(WIDTHS)
 STEPS = PIECES * KEY_BLOCKS
 VC_PITCH = 144
 AHEAD = 2
@@ -28,8 +29,9 @@ def tile_sdpasimple_kernel(tc, mask, q, kc, vc, offs, out):
     with (
         tc.tile_pool(name="held", bufs=1) as held,
         tc.tile_pool(name="work", bufs=4) as work,
-        tc.psum_pool(name="score_banks", bufs=3) as score_banks,
-        tc.psum_pool(name="product_banks", bufs=1) as product_banks,
+        tc.psum_pool(name="score_banks", bufs=2) as score_banks,
+        tc.psum_pool(name="product_banks", bufs=4) as product_banks,
+        tc.psum_pool(name="out_banks", bufs=2) as out_banks,
     ):
         offsets = held.tile([P, N // 16], U16, name="offsets")
         nc.sync.dma_start(offsets[:], offs)
@@ -43,10 +45,10 @@ def tile_sdpasimple_kernel(tc, mask, q, kc, vc, offs, out):
         vc_ones = held.tile([P, KEY_BLOCKS, VC_PITCH], BF16, name="vc_ones")
         nc.gpsimd.memset(vc_ones[:, :, D:VC_PITCH], 1.0)
         nc.scalar.dma_start(kc_sb[:, 0 : T // 2], kc[:, 0 : T // 2])
-        nc.scalar.dma_start(q_sb[:, 0:PIECE], q[:, 0:PIECE])
+        nc.scalar.dma_start(q_sb[:, 0:BANK], q[:, 0:BANK])
         nc.scalar.dma_start(vc_ones[:, :, 0:D], vc.rearrange("(b p) d -> p b d", p=P))
         nc.scalar.dma_start(kc_sb[:, T // 2 : T], kc[:, T // 2 : T])
-        nc.scalar.dma_start(q_sb[:, PIECE:N], q[:, PIECE:N])
+        nc.scalar.dma_start(q_sb[:, BANK:N], q[:, BANK:N])
         identity = held.tile([P, P], F32, name="identity")
         make_identity(nc, identity[:])
 
@@ -55,37 +57,38 @@ def tile_sdpasimple_kernel(tc, mask, q, kc, vc, offs, out):
 
         def scores(step):
             piece, b = divmod(step, KEY_BLOCKS)
-            score_ps = score_banks.tile([P, PIECE], F32, name="score_ps")
+            start, width = STARTS[piece], WIDTHS[piece]
+            score_ps = score_banks.tile([P, width], F32, name="score_ps")
             nc.tensor.matmul(
                 score_ps[:],
                 kc_sb[:, b * P : (b + 1) * P],
-                q_sb[:, piece * PIECE : (piece + 1) * PIECE],
+                q_sb[:, start : start + width],
                 start=True,
                 stop=True,
             )
-            scaled_sb = work.tile([P, PIECE], F32, name="scaled_sb")
+            scaled_sb = work.tile([P, width], F32, name="scaled_sb")
             nc.scalar.activation(scaled_sb[:], score_ps[:], COPY, scale=SCALE)
             scaled[step] = scaled_sb
 
         def weights(step):
             piece, b = divmod(step, KEY_BLOCKS)
-            cols = PIECE // 16
-            w_sb = work.tile([P, PIECE], F32, name="w_sb")
+            start, width = STARTS[piece], WIDTHS[piece]
+            w_sb = work.tile([P, width], F32, name="w_sb")
             nc.vector.tensor_tensor(
                 w_sb[:],
-                mask_sb[b][:].indirect(offsets[:, piece * cols : (piece + 1) * cols]),
+                mask_sb[b][:].indirect(offsets[:, start // 16 : (start + width) // 16]),
                 scaled.pop(step)[:],
                 ADD,
             )
-            e_sb = work.tile([P, PIECE], BF16, name="e_sb")
+            e_sb = work.tile([P, width], BF16, name="e_sb")
             nc.scalar.activation(e_sb[:], w_sb[:], EXP)
             if b == 0:
                 products[piece] = [
-                    product_banks.tile([P, D + 1], F32, name=f"product{c}") for c in range(SUBS)
+                    product_banks.tile([P, D + 1], F32, name="product") for c in range(width // P)
                 ]
-            for c in range(SUBS):
+            for c, product in enumerate(products[piece]):
                 nc.tensor.matmul(
-                    products[piece][c][:],
+                    product[:],
                     e_sb[:, c * P : (c + 1) * P],
                     vc_ones[:, b, 0 : D + 1],
                     start=(b == 0),
@@ -93,16 +96,17 @@ def tile_sdpasimple_kernel(tc, mask, q, kc, vc, offs, out):
                 )
 
         def finish(piece):
-            out_ps = product_banks.tile([D, PIECE], F32, name="out_ps")
+            start, width = STARTS[piece], WIDTHS[piece]
+            out_ps = out_banks.tile([D, width], F32, name="out_ps")
             for c, product in enumerate(products.pop(piece)):
                 inverse = work.tile([P, 1], F32, name="inverse")
                 nc.vector.reciprocal(inverse[:], product[:, D : D + 1])
                 normal = work.tile([P, D], F32, name="normal")
                 nc.scalar.activation(normal[:], product[:, 0:D], COPY, scale=inverse[:])
                 nc.tensor.transpose(out_ps[:, c * P : (c + 1) * P], normal[:], identity[:])
-            out_sb = work.tile([D, PIECE], F32, name="out_sb")
+            out_sb = work.tile([D, width], F32, name="out_sb")
             nc.vector.tensor_copy(out_sb[:], out_ps[:])
-            nc.sync.dma_start(out[:, piece * PIECE : (piece + 1) * PIECE], out_sb[:])
+            nc.sync.dma_start(out[:, start : start + width], out_sb[:])
 
         for step in range(AHEAD):
             scores(step)

@@ -14,13 +14,14 @@ P = 128
 D, T, S, N = 128, 1024, 1024, 1024
 SCALE = 1.0 / math.sqrt(D)
 KEY_BLOCKS = T // P
-BANK = 512
-WIDTHS = (BANK, N - BANK - P, P)
-STARTS = (0, BANK, N - P)
-PIECES = len(WIDTHS)
+PIECE = 512
+PIECES = N // PIECE
+SUBS = PIECE // P
 STEPS = PIECES * KEY_BLOCKS
 VC_PITCH = 144
 AHEAD = 2
+NORMALISE_LAG = 2
+STORE_LAG = 4
 FLOPS = 4 * D * T * N
 
 
@@ -28,85 +29,86 @@ def tile_sdpasimple_kernel(tc, mask, q, kc, vc, offs, out):
     nc = tc.nc
     with (
         tc.tile_pool(name="held", bufs=1) as held,
-        tc.tile_pool(name="work", bufs=4) as work,
-        tc.psum_pool(name="score_banks", bufs=2) as score_banks,
-        tc.psum_pool(name="product_banks", bufs=4) as product_banks,
-        tc.psum_pool(name="out_banks", bufs=2) as out_banks,
+        tc.tile_pool(name="work", bufs=6) as work,
+        tc.psum_pool(name="score_banks", bufs=3) as score_banks,
+        tc.psum_pool(name="product_banks", bufs=1) as product_banks,
     ):
         offsets = held.tile([P, N // 16], U16, name="offsets")
+        kc_sb = held.tile([D, T], BF16, name="kc_sb")
+        q_sb = held.tile([D, N], BF16, name="q_sb")
         nc.sync.dma_start(offsets[:], offs)
+        nc.sync.dma_start(kc_sb[:, 0 : T // 2], kc[:, 0 : T // 2])
+        nc.sync.dma_start(q_sb[:, 0:PIECE], q[:, 0:PIECE])
         mask_sb = []
         for b in range(KEY_BLOCKS):
             window = held.tile([P, S], F32, name=f"mask{b}")
             nc.sync.dma_start(window[:], mask[b * P : (b + 1) * P, :])
             mask_sb.append(window)
-        kc_sb = held.tile([D, T], BF16, name="kc_sb")
-        q_sb = held.tile([D, N], BF16, name="q_sb")
         vc_ones = held.tile([P, KEY_BLOCKS, VC_PITCH], BF16, name="vc_ones")
         nc.gpsimd.memset(vc_ones[:, :, D:VC_PITCH], 1.0)
-        nc.scalar.dma_start(kc_sb[:, 0 : T // 2], kc[:, 0 : T // 2])
-        nc.scalar.dma_start(q_sb[:, 0:BANK], q[:, 0:BANK])
         nc.scalar.dma_start(vc_ones[:, :, 0:D], vc.rearrange("(b p) d -> p b d", p=P))
         nc.scalar.dma_start(kc_sb[:, T // 2 : T], kc[:, T // 2 : T])
-        nc.scalar.dma_start(q_sb[:, BANK:N], q[:, BANK:N])
+        nc.scalar.dma_start(q_sb[:, PIECE:N], q[:, PIECE:N])
         identity = held.tile([P, P], F32, name="identity")
         make_identity(nc, identity[:])
 
         scaled = {}
         products = {}
+        out_tiles = {}
 
         def scores(step):
             piece, b = divmod(step, KEY_BLOCKS)
-            start, width = STARTS[piece], WIDTHS[piece]
-            score_ps = score_banks.tile([P, width], F32, name="score_ps")
+            score_ps = score_banks.tile([P, PIECE], F32, name="score_ps")
             nc.tensor.matmul(
                 score_ps[:],
                 kc_sb[:, b * P : (b + 1) * P],
-                q_sb[:, start : start + width],
+                q_sb[:, piece * PIECE : (piece + 1) * PIECE],
                 start=True,
                 stop=True,
             )
-            scaled_sb = work.tile([P, width], F32, name="scaled_sb")
+            scaled_sb = work.tile([P, PIECE], F32, name="scaled_sb")
             nc.scalar.activation(scaled_sb[:], score_ps[:], COPY, scale=SCALE)
             scaled[step] = scaled_sb
 
         def weights(step):
             piece, b = divmod(step, KEY_BLOCKS)
-            start, width = STARTS[piece], WIDTHS[piece]
-            w_sb = work.tile([P, width], F32, name="w_sb")
+            cols = PIECE // 16
+            w_sb = work.tile([P, PIECE], F32, name="w_sb")
             nc.vector.tensor_tensor(
                 w_sb[:],
-                mask_sb[b][:].indirect(offsets[:, start // 16 : (start + width) // 16]),
+                mask_sb[b][:].indirect(offsets[:, piece * cols : (piece + 1) * cols]),
                 scaled.pop(step)[:],
                 ADD,
             )
-            e_sb = work.tile([P, width], BF16, name="e_sb")
+            e_sb = work.tile([P, PIECE], BF16, name="e_sb")
             nc.scalar.activation(e_sb[:], w_sb[:], EXP)
             if b == 0:
                 products[piece] = [
-                    product_banks.tile([P, D + 1], F32, name="product") for c in range(width // P)
+                    product_banks.tile([P, D + 1], F32, name=f"product{c}") for c in range(SUBS)
                 ]
-            for c, product in enumerate(products[piece]):
+            for c in range(SUBS):
                 nc.tensor.matmul(
-                    product[:],
+                    products[piece][c][:],
                     e_sb[:, c * P : (c + 1) * P],
                     vc_ones[:, b, 0 : D + 1],
                     start=(b == 0),
                     stop=(b == KEY_BLOCKS - 1),
                 )
 
-        def finish(piece):
-            start, width = STARTS[piece], WIDTHS[piece]
-            out_ps = out_banks.tile([D, width], F32, name="out_ps")
+        def normalise(piece):
+            out_ps = product_banks.tile([D, PIECE], F32, name="out_ps")
             for c, product in enumerate(products.pop(piece)):
                 inverse = work.tile([P, 1], F32, name="inverse")
                 nc.vector.reciprocal(inverse[:], product[:, D : D + 1])
                 normal = work.tile([P, D], F32, name="normal")
                 nc.scalar.activation(normal[:], product[:, 0:D], COPY, scale=inverse[:])
                 nc.tensor.transpose(out_ps[:, c * P : (c + 1) * P], normal[:], identity[:])
-            out_sb = work.tile([D, width], F32, name="out_sb")
-            nc.vector.tensor_copy(out_sb[:], out_ps[:])
-            nc.sync.dma_start(out[:, start : start + width], out_sb[:])
+            out_tiles[piece] = out_ps
+
+        def store(piece):
+            out_sb = work.tile([D, PIECE], F32, name="out_sb")
+            nc.vector.tensor_copy(out_sb[:], out_tiles.pop(piece)[:])
+            nc.sync.dma_start(out[:, piece * PIECE : (piece + 1) * PIECE], out_sb[:])
 
         for step in range(AHEAD):
             scores(step)
@@ -114,6 +116,9 @@ def tile_sdpasimple_kernel(tc, mask, q, kc, vc, offs, out):
             if step + AHEAD < STEPS:
                 scores(step + AHEAD)
             weights(step)
-            if step >= KEY_BLOCKS and step % KEY_BLOCKS == AHEAD:
-                finish(step // KEY_BLOCKS - 1)
-        finish(PIECES - 1)
+            if step >= KEY_BLOCKS and (step - NORMALISE_LAG) % KEY_BLOCKS == KEY_BLOCKS - 1:
+                normalise((step - NORMALISE_LAG) // KEY_BLOCKS)
+            if step >= KEY_BLOCKS and (step - STORE_LAG) % KEY_BLOCKS == KEY_BLOCKS - 1:
+                store((step - STORE_LAG) // KEY_BLOCKS)
+        normalise(PIECES - 1)
+        store(PIECES - 1)

@@ -14,15 +14,20 @@ P = 128
 D, T, S, N = 128, 1024, 1024, 1024
 SCALE = 1.0 / math.sqrt(D)
 KEY_BLOCKS = T // P
-PIECE = 512
-PIECES = N // PIECE
-SUBS = PIECE // P
-STEPS = PIECES * KEY_BLOCKS
+BANK = 512
+WIDTHS = (512, 256, 128, 128)
+STARTS = (0, 512, 768, 896)
 VC_PITCH = 144
 AHEAD = 2
 NORMALISE_LAG = 2
 STORE_LAG = 4
 FLOPS = 4 * D * T * N
+
+GROUPS = [
+    (piece, first)
+    for piece, width in enumerate(WIDTHS)
+    for first in range(0, KEY_BLOCKS, BANK // width)
+]
 
 
 def tile_sdpasimple_kernel(tc, mask, q, kc, vc, offs, out):
@@ -30,15 +35,16 @@ def tile_sdpasimple_kernel(tc, mask, q, kc, vc, offs, out):
     with (
         tc.tile_pool(name="held", bufs=1) as held,
         tc.tile_pool(name="work", bufs=6) as work,
-        tc.psum_pool(name="score_banks", bufs=3) as score_banks,
-        tc.psum_pool(name="product_banks", bufs=1) as product_banks,
+        tc.psum_pool(name="score_banks", bufs=2) as score_banks,
+        tc.psum_pool(name="product_banks", bufs=4) as product_banks,
+        tc.psum_pool(name="out_banks", bufs=2) as out_banks,
     ):
         offsets = held.tile([P, N // 16], U16, name="offsets")
         kc_sb = held.tile([D, T], BF16, name="kc_sb")
         q_sb = held.tile([D, N], BF16, name="q_sb")
         nc.sync.dma_start(offsets[:], offs)
-        nc.sync.dma_start(kc_sb[:, 0 : T // 2], kc[:, 0 : T // 2])
-        nc.sync.dma_start(q_sb[:, 0:PIECE], q[:, 0:PIECE])
+        nc.scalar.dma_start(kc_sb[:, 0 : T // 2], kc[:, 0 : T // 2])
+        nc.sync.dma_start(q_sb[:, 0 : N // 2], q[:, 0 : N // 2])
         mask_sb = []
         for b in range(KEY_BLOCKS):
             window = held.tile([P, S], F32, name=f"mask{b}")
@@ -46,9 +52,9 @@ def tile_sdpasimple_kernel(tc, mask, q, kc, vc, offs, out):
             mask_sb.append(window)
         vc_ones = held.tile([P, KEY_BLOCKS, VC_PITCH], BF16, name="vc_ones")
         nc.gpsimd.memset(vc_ones[:, :, D:VC_PITCH], 1.0)
-        nc.scalar.dma_start(vc_ones[:, :, 0:D], vc.rearrange("(b p) d -> p b d", p=P))
         nc.scalar.dma_start(kc_sb[:, T // 2 : T], kc[:, T // 2 : T])
-        nc.scalar.dma_start(q_sb[:, PIECE:N], q[:, PIECE:N])
+        nc.scalar.dma_start(vc_ones[:, :, 0:D], vc.rearrange("(b p) d -> p b d", p=P))
+        nc.scalar.dma_start(q_sb[:, N // 2 : N], q[:, N // 2 : N])
         identity = held.tile([P, P], F32, name="identity")
         make_identity(nc, identity[:])
 
@@ -56,47 +62,54 @@ def tile_sdpasimple_kernel(tc, mask, q, kc, vc, offs, out):
         products = {}
         out_tiles = {}
 
-        def scores(step):
-            piece, b = divmod(step, KEY_BLOCKS)
-            score_ps = score_banks.tile([P, PIECE], F32, name="score_ps")
-            nc.tensor.matmul(
-                score_ps[:],
-                kc_sb[:, b * P : (b + 1) * P],
-                q_sb[:, piece * PIECE : (piece + 1) * PIECE],
-                start=True,
-                stop=True,
-            )
-            scaled_sb = work.tile([P, PIECE], F32, name="scaled_sb")
-            nc.scalar.activation(scaled_sb[:], score_ps[:], COPY, scale=SCALE)
-            scaled[step] = scaled_sb
-
-        def weights(step):
-            piece, b = divmod(step, KEY_BLOCKS)
-            cols = PIECE // 16
-            w_sb = work.tile([P, PIECE], F32, name="w_sb")
-            nc.vector.tensor_tensor(
-                w_sb[:],
-                mask_sb[b][:].indirect(offsets[:, piece * cols : (piece + 1) * cols]),
-                scaled.pop(step)[:],
-                ADD,
-            )
-            e_sb = work.tile([P, PIECE], BF16, name="e_sb")
-            nc.scalar.activation(e_sb[:], w_sb[:], EXP)
-            if b == 0:
-                products[piece] = [
-                    product_banks.tile([P, D + 1], F32, name=f"product{c}") for c in range(SUBS)
-                ]
-            for c in range(SUBS):
+        def scores(group):
+            piece, first = GROUPS[group]
+            start, width = STARTS[piece], WIDTHS[piece]
+            score_ps = score_banks.tile([P, BANK], F32, name="score_ps")
+            for i in range(BANK // width):
+                b = first + i
                 nc.tensor.matmul(
-                    products[piece][c][:],
-                    e_sb[:, c * P : (c + 1) * P],
-                    vc_ones[:, b, 0 : D + 1],
-                    start=(b == 0),
-                    stop=(b == KEY_BLOCKS - 1),
+                    score_ps[:, i * width : (i + 1) * width],
+                    kc_sb[:, b * P : (b + 1) * P],
+                    q_sb[:, start : start + width],
+                    start=True,
+                    stop=True,
                 )
+            scaled_sb = work.tile([P, BANK], F32, name="scaled_sb")
+            nc.scalar.activation(scaled_sb[:], score_ps[:], COPY, scale=SCALE)
+            scaled[group] = scaled_sb
+
+        def weights(group):
+            piece, first = GROUPS[group]
+            start, width = STARTS[piece], WIDTHS[piece]
+            scaled_sb = scaled.pop(group)
+            w_sb = work.tile([P, BANK], F32, name="w_sb")
+            for i in range(BANK // width):
+                nc.vector.tensor_tensor(
+                    w_sb[:, i * width : (i + 1) * width],
+                    mask_sb[first + i][:].indirect(offsets[:, start // 16 : (start + width) // 16]),
+                    scaled_sb[:, i * width : (i + 1) * width],
+                    ADD,
+                )
+            e_sb = work.tile([P, BANK], BF16, name="e_sb")
+            nc.scalar.activation(e_sb[:], w_sb[:], EXP)
+            if first == 0:
+                products[piece] = [
+                    product_banks.tile([P, D + 1], F32, name="product") for c in range(width // P)
+                ]
+            for i in range(BANK // width):
+                b = first + i
+                for c, product in enumerate(products[piece]):
+                    nc.tensor.matmul(
+                        product[:],
+                        e_sb[:, i * width + c * P : i * width + (c + 1) * P],
+                        vc_ones[:, b, 0 : D + 1],
+                        start=(b == 0),
+                        stop=(b == KEY_BLOCKS - 1),
+                    )
 
         def normalise(piece):
-            out_ps = product_banks.tile([D, PIECE], F32, name="out_ps")
+            out_ps = out_banks.tile([D, WIDTHS[piece]], F32, name="out_ps")
             for c, product in enumerate(products.pop(piece)):
                 inverse = work.tile([P, 1], F32, name="inverse")
                 nc.vector.reciprocal(inverse[:], product[:, D : D + 1])
@@ -106,19 +119,19 @@ def tile_sdpasimple_kernel(tc, mask, q, kc, vc, offs, out):
             out_tiles[piece] = out_ps
 
         def store(piece):
-            out_sb = work.tile([D, PIECE], F32, name="out_sb")
+            start, width = STARTS[piece], WIDTHS[piece]
+            out_sb = work.tile([D, width], F32, name="out_sb")
             nc.vector.tensor_copy(out_sb[:], out_tiles.pop(piece)[:])
-            nc.sync.dma_start(out[:, piece * PIECE : (piece + 1) * PIECE], out_sb[:])
+            nc.sync.dma_start(out[:, start : start + width], out_sb[:])
 
-        for step in range(AHEAD):
-            scores(step)
-        for step in range(STEPS):
-            if step + AHEAD < STEPS:
-                scores(step + AHEAD)
-            weights(step)
-            if step >= KEY_BLOCKS and (step - NORMALISE_LAG) % KEY_BLOCKS == KEY_BLOCKS - 1:
-                normalise((step - NORMALISE_LAG) // KEY_BLOCKS)
-            if step >= KEY_BLOCKS and (step - STORE_LAG) % KEY_BLOCKS == KEY_BLOCKS - 1:
-                store((step - STORE_LAG) // KEY_BLOCKS)
-        normalise(PIECES - 1)
-        store(PIECES - 1)
+        for group in range(AHEAD):
+            scores(group)
+        for group in range(len(GROUPS) + STORE_LAG):
+            if group + AHEAD < len(GROUPS):
+                scores(group + AHEAD)
+            if group < len(GROUPS):
+                weights(group)
+            for lag, end_of_piece in ((NORMALISE_LAG, normalise), (STORE_LAG, store)):
+                done = group - lag
+                if 0 <= done < len(GROUPS) and (done + 1 == len(GROUPS) or GROUPS[done + 1][1] == 0):
+                    end_of_piece(GROUPS[done][0])

@@ -14,29 +14,22 @@ P = 128
 D, T, S, N = 128, 1024, 1024, 1024
 SCALE = 1.0 / math.sqrt(D)
 KEY_BLOCKS = T // P
-BANK = 512
-WIDTHS = (512, 256, 128, 128)
-STARTS = (0, 512, 768, 896)
+PIECE = 512
+PIECES = N // PIECE
+SUBS = PIECE // P
+STEPS = PIECES * KEY_BLOCKS
 VC_PITCH = 144
-AHEAD = 2
-NORMALISE_LAG = 2
-STORE_LAG = 4
+AHEAD = 4
 FLOPS = 4 * D * T * N
-
-GROUPS = [
-    (piece, first)
-    for piece, width in enumerate(WIDTHS)
-    for first in range(0, KEY_BLOCKS, BANK // width)
-]
 
 
 def tile_sdpasimple_kernel(tc, mask, q, kc, vc, offs, out):
     nc = tc.nc
     with (
         tc.tile_pool(name="held", bufs=1) as held,
-        tc.tile_pool(name="work", bufs=6) as work,
+        tc.tile_pool(name="work", bufs=8) as work,
         tc.psum_pool(name="score_banks", bufs=2) as score_banks,
-        tc.psum_pool(name="product_banks", bufs=4) as product_banks,
+        tc.psum_pool(name="product_banks", bufs=1) as product_banks,
         tc.psum_pool(name="out_banks", bufs=2) as out_banks,
     ):
         offsets = held.tile([P, N // 16], U16, name="offsets")
@@ -44,7 +37,7 @@ def tile_sdpasimple_kernel(tc, mask, q, kc, vc, offs, out):
         q_sb = held.tile([D, N], BF16, name="q_sb")
         nc.sync.dma_start(offsets[:], offs)
         nc.scalar.dma_start(kc_sb[:, 0 : T // 2], kc[:, 0 : T // 2])
-        nc.sync.dma_start(q_sb[:, 0 : N // 2], q[:, 0 : N // 2])
+        nc.sync.dma_start(q_sb[:, 0:PIECE], q[:, 0:PIECE])
         mask_sb = []
         for b in range(KEY_BLOCKS):
             window = held.tile([P, S], F32, name=f"mask{b}")
@@ -54,84 +47,79 @@ def tile_sdpasimple_kernel(tc, mask, q, kc, vc, offs, out):
         nc.gpsimd.memset(vc_ones[:, :, D:VC_PITCH], 1.0)
         nc.scalar.dma_start(kc_sb[:, T // 2 : T], kc[:, T // 2 : T])
         nc.scalar.dma_start(vc_ones[:, :, 0:D], vc.rearrange("(b p) d -> p b d", p=P))
-        nc.scalar.dma_start(q_sb[:, N // 2 : N], q[:, N // 2 : N])
+        nc.scalar.dma_start(q_sb[:, PIECE:N], q[:, PIECE:N])
         identity = held.tile([P, P], F32, name="identity")
         make_identity(nc, identity[:])
 
         scaled = {}
         products = {}
-        out_tiles = {}
 
-        def scores(group):
-            piece, first = GROUPS[group]
-            start, width = STARTS[piece], WIDTHS[piece]
-            score_ps = score_banks.tile([P, BANK], F32, name="score_ps")
-            for i in range(BANK // width):
-                b = first + i
-                nc.tensor.matmul(
-                    score_ps[:, i * width : (i + 1) * width],
-                    kc_sb[:, b * P : (b + 1) * P],
-                    q_sb[:, start : start + width],
-                    start=True,
-                    stop=True,
-                )
-            scaled_sb = work.tile([P, BANK], F32, name="scaled_sb")
+        def scores(step):
+            piece, b = divmod(step, KEY_BLOCKS)
+            score_ps = score_banks.tile([P, PIECE], F32, name="score_ps")
+            nc.tensor.matmul(
+                score_ps[:],
+                kc_sb[:, b * P : (b + 1) * P],
+                q_sb[:, piece * PIECE : (piece + 1) * PIECE],
+                start=True,
+                stop=True,
+            )
+            scaled_sb = work.tile([P, PIECE], F32, name="scaled_sb")
             nc.scalar.activation(scaled_sb[:], score_ps[:], COPY, scale=SCALE)
-            scaled[group] = scaled_sb
+            scaled[step] = scaled_sb
 
-        def weights(group):
-            piece, first = GROUPS[group]
-            start, width = STARTS[piece], WIDTHS[piece]
-            scaled_sb = scaled.pop(group)
-            w_sb = work.tile([P, BANK], F32, name="w_sb")
-            for i in range(BANK // width):
-                nc.vector.tensor_tensor(
-                    w_sb[:, i * width : (i + 1) * width],
-                    mask_sb[first + i][:].indirect(offsets[:, start // 16 : (start + width) // 16]),
-                    scaled_sb[:, i * width : (i + 1) * width],
-                    ADD,
-                )
-            e_sb = work.tile([P, BANK], BF16, name="e_sb")
+        def weights(step):
+            piece, b = divmod(step, KEY_BLOCKS)
+            cols = PIECE // 16
+            w_sb = work.tile([P, PIECE], F32, name="w_sb")
+            nc.vector.tensor_tensor(
+                w_sb[:],
+                mask_sb[b][:].indirect(offsets[:, piece * cols : (piece + 1) * cols]),
+                scaled.pop(step)[:],
+                ADD,
+            )
+            e_sb = work.tile([P, PIECE], BF16, name="e_sb")
             nc.scalar.activation(e_sb[:], w_sb[:], EXP)
-            if first == 0:
+            if b == 0:
                 products[piece] = [
-                    product_banks.tile([P, D + 1], F32, name="product") for c in range(width // P)
+                    product_banks.tile([P, D + 1], F32, name=f"product{c}") for c in range(SUBS)
                 ]
-            for i in range(BANK // width):
-                b = first + i
-                for c, product in enumerate(products[piece]):
-                    nc.tensor.matmul(
-                        product[:],
-                        e_sb[:, i * width + c * P : i * width + (c + 1) * P],
-                        vc_ones[:, b, 0 : D + 1],
-                        start=(b == 0),
-                        stop=(b == KEY_BLOCKS - 1),
-                    )
+            for c in range(SUBS):
+                nc.tensor.matmul(
+                    products[piece][c][:],
+                    e_sb[:, c * P : (c + 1) * P],
+                    vc_ones[:, b, 0 : D + 1],
+                    start=(b == 0),
+                    stop=(b == KEY_BLOCKS - 1),
+                )
 
-        def normalise(piece):
-            out_ps = out_banks.tile([D, WIDTHS[piece]], F32, name="out_ps")
-            for c, product in enumerate(products.pop(piece)):
-                inverse = work.tile([P, 1], F32, name="inverse")
-                nc.vector.reciprocal(inverse[:], product[:, D : D + 1])
-                normal = work.tile([P, D], F32, name="normal")
-                nc.scalar.activation(normal[:], product[:, 0:D], COPY, scale=inverse[:])
-                nc.tensor.transpose(out_ps[:, c * P : (c + 1) * P], normal[:], identity[:])
-            out_tiles[piece] = out_ps
+        def finish(piece):
+            half_width = PIECE // 2
+            for half in range(2):
+                out_ps = out_banks.tile([D, half_width], F32, name="out_ps")
+                for i in range(SUBS // 2):
+                    product = products[piece][half * (SUBS // 2) + i]
+                    inverse = work.tile([P, 1], F32, name="inverse")
+                    nc.vector.reciprocal(inverse[:], product[:, D : D + 1])
+                    normal = work.tile([P, D], F32, name="normal")
+                    nc.scalar.activation(normal[:], product[:, 0:D], COPY, scale=inverse[:])
+                    nc.tensor.transpose(out_ps[:, i * P : (i + 1) * P], normal[:], identity[:])
+                out_sb = work.tile([D, half_width], F32, name="out_sb")
+                first = piece * PIECE + half * half_width
+                if half == 0:
+                    nc.vector.tensor_copy(out_sb[:], out_ps[:])
+                    nc.sync.dma_start(out[:, first : first + half_width], out_sb[:])
+                else:
+                    nc.scalar.copy(out_sb[:], out_ps[:])
+                    nc.scalar.dma_start(out[:, first : first + half_width], out_sb[:])
+            products.pop(piece)
 
-        def store(piece):
-            start, width = STARTS[piece], WIDTHS[piece]
-            out_sb = work.tile([D, width], F32, name="out_sb")
-            nc.vector.tensor_copy(out_sb[:], out_tiles.pop(piece)[:])
-            nc.sync.dma_start(out[:, start : start + width], out_sb[:])
-
-        for group in range(AHEAD):
-            scores(group)
-        for group in range(len(GROUPS) + STORE_LAG):
-            if group + AHEAD < len(GROUPS):
-                scores(group + AHEAD)
-            if group < len(GROUPS):
-                weights(group)
-            for lag, end_of_piece in ((NORMALISE_LAG, normalise), (STORE_LAG, store)):
-                done = group - lag
-                if 0 <= done < len(GROUPS) and (done + 1 == len(GROUPS) or GROUPS[done + 1][1] == 0):
-                    end_of_piece(GROUPS[done][0])
+        for step in range(AHEAD):
+            scores(step)
+        for step in range(STEPS):
+            if step + AHEAD < STEPS:
+                scores(step + AHEAD)
+            weights(step)
+            if step >= KEY_BLOCKS and step % KEY_BLOCKS == 2:
+                finish(step // KEY_BLOCKS - 1)
+        finish(PIECES - 1)

@@ -20,6 +20,7 @@ SUBS = PIECE // P
 STEPS = PIECES * KEY_BLOCKS
 VC_PITCH = 144
 AHEAD = 4
+LAST_CUTS = 2
 FLOPS = 4 * D * T * N
 
 
@@ -70,39 +71,50 @@ def tile_sdpasimple_kernel(tc, mask, q, kc, vc, offs, out):
 
         def weights(step):
             piece, b = divmod(step, KEY_BLOCKS)
-            cols = PIECE // 16
-            w_sb = work.tile([P, PIECE], F32, name="w_sb")
-            nc.vector.tensor_tensor(
-                w_sb[:],
-                mask_sb[b][:].indirect(offsets[:, piece * cols : (piece + 1) * cols]),
-                scaled.pop(step)[:],
-                ADD,
-            )
-            e_sb = work.tile([P, PIECE], BF16, name="e_sb")
-            nc.scalar.activation(e_sb[:], w_sb[:], EXP)
             if b == 0:
                 products[piece] = [
                     product_banks.tile([P, D + 1], F32, name=f"product{c}") for c in range(SUBS)
                 ]
-            for c in range(SUBS):
-                nc.tensor.matmul(
-                    products[piece][c][:],
-                    e_sb[:, c * P : (c + 1) * P],
-                    vc_ones[:, b, 0 : D + 1],
-                    start=(b == 0),
-                    stop=(b == KEY_BLOCKS - 1),
+            scaled_sb = scaled.pop(step)
+            w_sb = work.tile([P, PIECE], F32, name="w_sb")
+            e_sb = work.tile([P, PIECE], BF16, name="e_sb")
+            cuts = LAST_CUTS if step == STEPS - 1 else 1
+            width = PIECE // cuts
+            for cut in range(cuts):
+                lo, hi = cut * width, (cut + 1) * width
+                nc.vector.tensor_tensor(
+                    w_sb[:, lo:hi],
+                    mask_sb[b][:].indirect(
+                        offsets[:, (piece * PIECE + lo) // 16 : (piece * PIECE + hi) // 16]
+                    ),
+                    scaled_sb[:, lo:hi],
+                    ADD,
                 )
+                nc.scalar.activation(e_sb[:, lo:hi], w_sb[:, lo:hi], EXP)
+                for c in range(lo // P, hi // P):
+                    nc.tensor.matmul(
+                        products[piece][c][:],
+                        e_sb[:, c * P : (c + 1) * P],
+                        vc_ones[:, b, 0 : D + 1],
+                        start=(b == 0),
+                        stop=(b == KEY_BLOCKS - 1),
+                    )
 
         def finish(piece):
             half_width = PIECE // 2
+            inverses = []
+            for product in products[piece]:
+                inverse = work.tile([P, 1], F32, name="inverse")
+                nc.vector.reciprocal(inverse[:], product[:, D : D + 1])
+                inverses.append(inverse)
             for half in range(2):
                 out_ps = out_banks.tile([D, half_width], F32, name="out_ps")
                 for i in range(SUBS // 2):
-                    product = products[piece][half * (SUBS // 2) + i]
-                    inverse = work.tile([P, 1], F32, name="inverse")
-                    nc.vector.reciprocal(inverse[:], product[:, D : D + 1])
+                    c = half * (SUBS // 2) + i
                     normal = work.tile([P, D], F32, name="normal")
-                    nc.scalar.activation(normal[:], product[:, 0:D], COPY, scale=inverse[:])
+                    nc.scalar.activation(
+                        normal[:], products[piece][c][:, 0:D], COPY, scale=inverses[c][:]
+                    )
                     nc.tensor.transpose(out_ps[:, i * P : (i + 1) * P], normal[:], identity[:])
                 out_sb = work.tile([D, half_width], F32, name="out_sb")
                 first = piece * PIECE + half * half_width

@@ -16,11 +16,18 @@ SCALE = 1.0 / math.sqrt(D)
 KEY_BLOCKS = T // P
 PIECE = 512
 PIECES = N // PIECE
-SUBS = PIECE // P
+PAIR = 2
+PAIRS = PIECE // (PAIR * P)
 STEPS = PIECES * KEY_BLOCKS
-VC_PITCH = 144
+PITCH = 144
 AHEAD = 4
-LAST_CUTS = 2
+EARLY = 2
+ORDER = (
+    [(piece, b) for b in range(EARLY) for piece in range(PIECES)]
+    + [(0, b) for b in range(EARLY, KEY_BLOCKS)]
+    + [(1, b) for b in range(EARLY, KEY_BLOCKS)]
+)
+FIRST_DONE = ORDER.index((0, KEY_BLOCKS - 1))
 FLOPS = 4 * D * T * N
 
 
@@ -44,19 +51,22 @@ def tile_sdpasimple_kernel(tc, mask, q, kc, vc, offs, out):
             window = held.tile([P, S], F32, name=f"mask{b}")
             nc.sync.dma_start(window[:], mask[b * P : (b + 1) * P, :])
             mask_sb.append(window)
-        vc_ones = held.tile([P, KEY_BLOCKS, VC_PITCH], BF16, name="vc_ones")
-        nc.gpsimd.memset(vc_ones[:, :, D:VC_PITCH], 1.0)
+        vc_ones = held.tile([P, KEY_BLOCKS, PITCH], BF16, name="vc_ones")
+        nc.gpsimd.memset(vc_ones[:, :, D:PITCH], 1.0)
+        zeros = held.tile([P, P], BF16, name="zeros")
+        nc.gpsimd.memset(zeros[:], 0.0)
+        nc.scalar.dma_start(q_sb[:, PIECE:N], q[:, PIECE:N])
         nc.scalar.dma_start(kc_sb[:, T // 2 : T], kc[:, T // 2 : T])
         nc.scalar.dma_start(vc_ones[:, :, 0:D], vc.rearrange("(b p) d -> p b d", p=P))
-        nc.scalar.dma_start(q_sb[:, PIECE:N], q[:, PIECE:N])
         identity = held.tile([P, P], F32, name="identity")
         make_identity(nc, identity[:])
 
         scaled = {}
         products = {}
+        inverses = {}
+        turned = {}
 
-        def scores(step):
-            piece, b = divmod(step, KEY_BLOCKS)
+        def scores(piece, b):
             score_ps = score_banks.tile([P, PIECE], F32, name="score_ps")
             nc.tensor.matmul(
                 score_ps[:],
@@ -67,18 +77,13 @@ def tile_sdpasimple_kernel(tc, mask, q, kc, vc, offs, out):
             )
             scaled_sb = work.tile([P, PIECE], F32, name="scaled_sb")
             nc.scalar.activation(scaled_sb[:], score_ps[:], COPY, scale=SCALE)
-            scaled[step] = scaled_sb
+            scaled[piece, b] = scaled_sb
 
-        def weights(step):
-            piece, b = divmod(step, KEY_BLOCKS)
-            if b == 0:
-                products[piece] = [
-                    product_banks.tile([P, D + 1], F32, name=f"product{c}") for c in range(SUBS)
-                ]
-            scaled_sb = scaled.pop(step)
+        def weights(piece, b):
+            scaled_sb = scaled.pop((piece, b))
             w_sb = work.tile([P, PIECE], F32, name="w_sb")
             e_sb = work.tile([P, PIECE], BF16, name="e_sb")
-            cuts = LAST_CUTS if step == STEPS - 1 else 1
+            cuts = PAIRS if (piece, b) == ORDER[-1] else 1
             width = PIECE // cuts
             for cut in range(cuts):
                 lo, hi = cut * width, (cut + 1) * width
@@ -92,46 +97,66 @@ def tile_sdpasimple_kernel(tc, mask, q, kc, vc, offs, out):
                 )
                 nc.scalar.activation(e_sb[:, lo:hi], w_sb[:, lo:hi], EXP)
                 for c in range(lo // P, hi // P):
+                    pair, i = divmod(c, PAIR)
                     nc.tensor.matmul(
-                        products[piece][c][:],
+                        products[piece, pair][:, i, 0 : D + 1],
                         e_sb[:, c * P : (c + 1) * P],
                         vc_ones[:, b, 0 : D + 1],
-                        start=(b == 0),
-                        stop=(b == KEY_BLOCKS - 1),
+                        start=False,
+                        stop=(b == KEY_BLOCKS - 1 and i == PAIR - 1),
                     )
 
-        def finish(piece):
-            half_width = PIECE // 2
-            inverses = []
-            for product in products[piece]:
-                inverse = work.tile([P, 1], F32, name="inverse")
-                nc.vector.reciprocal(inverse[:], product[:, D : D + 1])
-                inverses.append(inverse)
-            for half in range(2):
-                out_ps = out_banks.tile([D, half_width], F32, name="out_ps")
-                for i in range(SUBS // 2):
-                    c = half * (SUBS // 2) + i
+        def invert(piece):
+            for pair in range(PAIRS):
+                inverse = work.tile([P, PAIR, 1], F32, name="inverse")
+                nc.vector.reciprocal(inverse[:], products[piece, pair][:, :, D : D + 1])
+                inverses[piece, pair] = inverse
+
+        def normalise(piece):
+            for pair in range(PAIRS):
+                out_ps = out_banks.tile([D, PAIR * P], F32, name="out_ps")
+                for i in range(PAIR):
                     normal = work.tile([P, D], F32, name="normal")
                     nc.scalar.activation(
-                        normal[:], products[piece][c][:, 0:D], COPY, scale=inverses[c][:]
+                        normal[:],
+                        products[piece, pair][:, i, 0:D],
+                        COPY,
+                        scale=inverses[piece, pair][:, i, :],
                     )
                     nc.tensor.transpose(out_ps[:, i * P : (i + 1) * P], normal[:], identity[:])
-                out_sb = work.tile([D, half_width], F32, name="out_sb")
-                first = piece * PIECE + half * half_width
-                if half == 0:
-                    nc.vector.tensor_copy(out_sb[:], out_ps[:])
-                    nc.sync.dma_start(out[:, first : first + half_width], out_sb[:])
+                turned[piece, pair] = out_ps
+
+        def leave(piece, vector_helps):
+            for pair in range(PAIRS):
+                out_sb = work.tile([D, PAIR * P], F32, name="out_sb")
+                first = piece * PIECE + pair * PAIR * P
+                if pair == 0 and vector_helps:
+                    nc.vector.tensor_copy(out_sb[:], turned[piece, pair][:])
                 else:
-                    nc.scalar.copy(out_sb[:], out_ps[:])
-                    nc.scalar.dma_start(out[:, first : first + half_width], out_sb[:])
-            products.pop(piece)
+                    nc.scalar.copy(out_sb[:], turned[piece, pair][:])
+                nc.sync.dma_start(out[:, first : first + PAIR * P], out_sb[:])
 
         for step in range(AHEAD):
-            scores(step)
+            scores(*ORDER[step])
+
+        for piece in range(PIECES):
+            for pair in range(PAIRS):
+                product = product_banks.tile([P, PAIR, PITCH], F32, name=f"product{piece}_{pair}")
+                nc.tensor.matmul(
+                    product[:], zeros[:], q_sb[:, 0 : PAIR * PITCH], start=True, stop=False
+                )
+                products[piece, pair] = product
+
         for step in range(STEPS):
             if step + AHEAD < STEPS:
-                scores(step + AHEAD)
-            weights(step)
-            if step >= KEY_BLOCKS and step % KEY_BLOCKS == 2:
-                finish(step // KEY_BLOCKS - 1)
-        finish(PIECES - 1)
+                scores(*ORDER[step + AHEAD])
+            weights(*ORDER[step])
+            if step == FIRST_DONE + 2:
+                invert(0)
+            if step == FIRST_DONE + 3:
+                normalise(0)
+            if step == FIRST_DONE + 4:
+                leave(0, vector_helps=False)
+        invert(1)
+        normalise(1)
+        leave(1, vector_helps=True)

@@ -14,20 +14,13 @@ P = 128
 D, T, S, N = 128, 1024, 1024, 1024
 SCALE = 1.0 / math.sqrt(D)
 KEY_BLOCKS = T // P
-PIECE = 512
-PIECES = N // PIECE
+BANK = 512
 PAIR = 2
-PAIRS = PIECE // (PAIR * P)
-STEPS = PIECES * KEY_BLOCKS
+CUT = PAIR * P
+CUTS = N // CUT
 PITCH = 144
-AHEAD = 4
-EARLY = 2
-ORDER = (
-    [(piece, b) for b in range(EARLY) for piece in range(PIECES)]
-    + [(0, b) for b in range(EARLY, KEY_BLOCKS)]
-    + [(1, b) for b in range(EARLY, KEY_BLOCKS)]
-)
-FIRST_DONE = ORDER.index((0, KEY_BLOCKS - 1))
+AHEAD = 2
+LATE = 2
 FLOPS = 4 * D * T * N
 
 
@@ -35,17 +28,17 @@ def tile_sdpasimple_kernel(tc, mask, q, kc, vc, offs, out):
     nc = tc.nc
     with (
         tc.tile_pool(name="held", bufs=1) as held,
-        tc.tile_pool(name="work", bufs=8) as work,
-        tc.psum_pool(name="score_banks", bufs=2) as score_banks,
+        tc.tile_pool(name="work", bufs=4) as work,
+        tc.tile_pool(name="small", bufs=8) as small,
         tc.psum_pool(name="product_banks", bufs=1) as product_banks,
-        tc.psum_pool(name="out_banks", bufs=2) as out_banks,
+        tc.psum_pool(name="other_banks", bufs=4) as other_banks,
     ):
         offsets = held.tile([P, N // 16], U16, name="offsets")
         kc_sb = held.tile([D, T], BF16, name="kc_sb")
         q_sb = held.tile([D, N], BF16, name="q_sb")
         nc.sync.dma_start(offsets[:], offs)
         nc.scalar.dma_start(kc_sb[:, 0 : T // 2], kc[:, 0 : T // 2])
-        nc.sync.dma_start(q_sb[:, 0:PIECE], q[:, 0:PIECE])
+        nc.sync.dma_start(q_sb[:, 0:BANK], q[:, 0:BANK])
         mask_sb = []
         for b in range(KEY_BLOCKS):
             window = held.tile([P, S], F32, name=f"mask{b}")
@@ -55,108 +48,84 @@ def tile_sdpasimple_kernel(tc, mask, q, kc, vc, offs, out):
         nc.gpsimd.memset(vc_ones[:, :, D:PITCH], 1.0)
         zeros = held.tile([P, P], BF16, name="zeros")
         nc.gpsimd.memset(zeros[:], 0.0)
-        nc.scalar.dma_start(q_sb[:, PIECE:N], q[:, PIECE:N])
+        nc.scalar.dma_start(q_sb[:, BANK:N], q[:, BANK:N])
         nc.scalar.dma_start(kc_sb[:, T // 2 : T], kc[:, T // 2 : T])
         nc.scalar.dma_start(vc_ones[:, :, 0:D], vc.rearrange("(b p) d -> p b d", p=P))
         identity = held.tile([P, P], F32, name="identity")
         make_identity(nc, identity[:])
 
         scaled = {}
-        products = {}
+        products = []
         inverses = {}
         turned = {}
 
-        def scores(piece, b):
-            score_ps = score_banks.tile([P, PIECE], F32, name="score_ps")
-            nc.tensor.matmul(
-                score_ps[:],
-                kc_sb[:, b * P : (b + 1) * P],
-                q_sb[:, piece * PIECE : (piece + 1) * PIECE],
-                start=True,
-                stop=True,
-            )
-            scaled_sb = work.tile([P, PIECE], F32, name="scaled_sb")
-            nc.scalar.activation(scaled_sb[:], score_ps[:], COPY, scale=SCALE)
-            scaled[piece, b] = scaled_sb
-
-        def weights(piece, b):
-            scaled_sb = scaled.pop((piece, b))
-            w_sb = work.tile([P, PIECE], F32, name="w_sb")
-            e_sb = work.tile([P, PIECE], BF16, name="e_sb")
-            cuts = PAIRS if (piece, b) == ORDER[-1] else 1
-            width = PIECE // cuts
-            for cut in range(cuts):
-                lo, hi = cut * width, (cut + 1) * width
-                nc.vector.tensor_tensor(
-                    w_sb[:, lo:hi],
-                    mask_sb[b][:].indirect(
-                        offsets[:, (piece * PIECE + lo) // 16 : (piece * PIECE + hi) // 16]
-                    ),
-                    scaled_sb[:, lo:hi],
-                    ADD,
-                )
-                nc.scalar.activation(e_sb[:, lo:hi], w_sb[:, lo:hi], EXP)
-                for c in range(lo // P, hi // P):
-                    pair, i = divmod(c, PAIR)
-                    nc.tensor.matmul(
-                        products[piece, pair][:, i, 0 : D + 1],
-                        e_sb[:, c * P : (c + 1) * P],
-                        vc_ones[:, b, 0 : D + 1],
-                        start=False,
-                        stop=(b == KEY_BLOCKS - 1 and i == PAIR - 1),
-                    )
-
-        def invert(piece):
-            for pair in range(PAIRS):
-                inverse = work.tile([P, PAIR, 1], F32, name="inverse")
-                nc.vector.reciprocal(inverse[:], products[piece, pair][:, :, D : D + 1])
-                inverses[piece, pair] = inverse
-
-        def normalise(piece):
-            for pair in range(PAIRS):
-                out_ps = out_banks.tile([D, PAIR * P], F32, name="out_ps")
-                for i in range(PAIR):
-                    normal = work.tile([P, D], F32, name="normal")
-                    nc.scalar.activation(
-                        normal[:],
-                        products[piece, pair][:, i, 0:D],
-                        COPY,
-                        scale=inverses[piece, pair][:, i, :],
-                    )
-                    nc.tensor.transpose(out_ps[:, i * P : (i + 1) * P], normal[:], identity[:])
-                turned[piece, pair] = out_ps
-
-        def leave(piece, vector_helps):
-            for pair in range(PAIRS):
-                out_sb = work.tile([D, PAIR * P], F32, name="out_sb")
-                first = piece * PIECE + pair * PAIR * P
-                if pair == 0 and vector_helps:
-                    nc.vector.tensor_copy(out_sb[:], turned[piece, pair][:])
-                else:
-                    nc.scalar.copy(out_sb[:], turned[piece, pair][:])
-                nc.sync.dma_start(out[:, first : first + PAIR * P], out_sb[:])
-
-        for step in range(AHEAD):
-            scores(*ORDER[step])
-
-        for piece in range(PIECES):
-            for pair in range(PAIRS):
-                product = product_banks.tile([P, PAIR, PITCH], F32, name=f"product{piece}_{pair}")
+        def scores(b):
+            scaled_sb = work.tile([P, N], F32, name="scaled_sb")
+            for lo in range(0, N, BANK):
+                score_ps = other_banks.tile([P, BANK], F32, name="score_ps", tag="bank")
                 nc.tensor.matmul(
-                    product[:], zeros[:], q_sb[:, 0 : PAIR * PITCH], start=True, stop=False
+                    score_ps[:],
+                    kc_sb[:, b * P : (b + 1) * P],
+                    q_sb[:, lo : lo + BANK],
+                    start=True,
+                    stop=True,
                 )
-                products[piece, pair] = product
+                nc.scalar.activation(scaled_sb[:, lo : lo + BANK], score_ps[:], COPY, scale=SCALE)
+            scaled[b] = scaled_sb
 
-        for step in range(STEPS):
-            if step + AHEAD < STEPS:
-                scores(*ORDER[step + AHEAD])
-            weights(*ORDER[step])
-            if step == FIRST_DONE + 2:
-                invert(0)
-            if step == FIRST_DONE + 3:
-                normalise(0)
-            if step == FIRST_DONE + 4:
-                leave(0, vector_helps=False)
-        invert(1)
-        normalise(1)
-        leave(1, vector_helps=True)
+        def weights(b, w_sb, e_sb, lo, hi):
+            nc.vector.tensor_tensor(
+                w_sb[:, lo:hi],
+                mask_sb[b][:].indirect(offsets[:, lo // 16 : hi // 16]),
+                scaled[b][:, lo:hi],
+                ADD,
+            )
+            nc.scalar.activation(e_sb[:, lo:hi], w_sb[:, lo:hi], EXP)
+            for c in range(lo // P, hi // P):
+                cut, i = divmod(c, PAIR)
+                nc.tensor.matmul(
+                    products[cut][:, i, 0 : D + 1],
+                    e_sb[:, c * P : (c + 1) * P],
+                    vc_ones[:, b, 0 : D + 1],
+                    start=False,
+                    stop=(b == KEY_BLOCKS - 1 and i == PAIR - 1),
+                )
+
+        def divide(cut):
+            inverse = small.tile([P, PAIR, 1], F32, name="inverse")
+            nc.vector.reciprocal(inverse[:], products[cut][:, :, D : D + 1])
+            out_ps = other_banks.tile([D, CUT], F32, name="out_ps", tag="bank")
+            for i in range(PAIR):
+                normal = small.tile([P, D], F32, name="normal")
+                nc.scalar.activation(
+                    normal[:], products[cut][:, i, 0:D], COPY, scale=inverse[:, i, :]
+                )
+                nc.tensor.transpose(out_ps[:, i * P : (i + 1) * P], normal[:], identity[:])
+            turned[cut] = out_ps
+
+        def leave(cut):
+            out_sb = small.tile([D, CUT], F32, name="out_sb")
+            nc.vector.tensor_copy(out_sb[:], turned[cut][:])
+            nc.sync.dma_start(out[:, cut * CUT : (cut + 1) * CUT], out_sb[:])
+
+        for b in range(AHEAD):
+            scores(b)
+        for cut in range(CUTS):
+            product = product_banks.tile([P, PAIR, PITCH], F32, name=f"product{cut}")
+            nc.tensor.matmul(product[:], zeros[:], q_sb[:, 0 : PAIR * PITCH], start=True, stop=False)
+            products.append(product)
+        for b in range(KEY_BLOCKS):
+            if b + AHEAD < KEY_BLOCKS:
+                scores(b + AHEAD)
+            w_sb = work.tile([P, N], F32, name="w_sb")
+            e_sb = work.tile([P, N], BF16, name="e_sb")
+            if b < KEY_BLOCKS - 1:
+                weights(b, w_sb, e_sb, 0, N)
+            else:
+                for cut in range(CUTS + LATE):
+                    if cut < CUTS:
+                        weights(b, w_sb, e_sb, cut * CUT, (cut + 1) * CUT)
+                    if cut >= LATE:
+                        divide(cut - LATE)
+        for cut in range(CUTS):
+            leave(cut)

@@ -36,21 +36,20 @@ def tile_sdpasimple_kernel(tc, mask, q, kc, vc, offs, out):
         offsets = held.tile([P, N // 16], U16, name="offsets")
         kc_sb = held.tile([D, T], BF16, name="kc_sb")
         q_sb = held.tile([D, N], BF16, name="q_sb")
-        nc.sync.dma_start(offsets[:], offs)
-        nc.scalar.dma_start(kc_sb[:, 0 : T // 2], kc[:, 0 : T // 2])
-        nc.sync.dma_start(q_sb[:, 0:BANK], q[:, 0:BANK])
-        mask_sb = []
-        for b in range(KEY_BLOCKS):
-            window = held.tile([P, S], F32, name=f"mask{b}")
-            nc.sync.dma_start(window[:], mask[b * P : (b + 1) * P, :])
-            mask_sb.append(window)
+        mask_sb = [held.tile([P, S], F32, name=f"mask{b}") for b in range(KEY_BLOCKS)]
         vc_ones = held.tile([P, KEY_BLOCKS, PITCH], BF16, name="vc_ones")
         nc.gpsimd.memset(vc_ones[:, :, D:PITCH], 1.0)
         zeros = held.tile([P, P], BF16, name="zeros")
         nc.gpsimd.memset(zeros[:], 0.0)
+        nc.sync.dma_start(offsets[:], offs)
+        nc.scalar.dma_start(kc_sb[:, 0 : T // 2], kc[:, 0 : T // 2])
+        nc.sync.dma_start(q_sb[:, 0:BANK], q[:, 0:BANK])
         nc.scalar.dma_start(q_sb[:, BANK:N], q[:, BANK:N])
-        nc.scalar.dma_start(kc_sb[:, T // 2 : T], kc[:, T // 2 : T])
-        nc.scalar.dma_start(vc_ones[:, :, 0:D], vc.rearrange("(b p) d -> p b d", p=P))
+        nc.sync.dma_start(mask_sb[0][:], mask[0:P, :])
+        nc.sync.dma_start(vc_ones[:, :, 0:D], vc.rearrange("(b p) d -> p b d", p=P))
+        nc.sync.dma_start(kc_sb[:, T // 2 : T], kc[:, T // 2 : T])
+        for b in range(1, KEY_BLOCKS):
+            nc.sync.dma_start(mask_sb[b][:], mask[b * P : (b + 1) * P, :])
         identity = held.tile([P, P], F32, name="identity")
         make_identity(nc, identity[:])
 
@@ -119,7 +118,10 @@ def tile_sdpasimple_kernel(tc, mask, q, kc, vc, offs, out):
                 scores(b + AHEAD)
             w_sb = work.tile([P, N], F32, name="w_sb")
             e_sb = work.tile([P, N], BF16, name="e_sb")
-            if b < KEY_BLOCKS - 1:
+            if b == 0:
+                for lo in range(0, N, BANK):
+                    weights(b, w_sb, e_sb, lo, lo + BANK)
+            elif b < KEY_BLOCKS - 1:
                 weights(b, w_sb, e_sb, 0, N)
             else:
                 for cut in range(CUTS + LATE):

@@ -42,12 +42,12 @@ def tile_sdpasimple_kernel(tc, mask, q, kc, vc, offs, out):
         zeros = held.tile([P, P], BF16, name="zeros")
         nc.gpsimd.memset(zeros[:], 0.0)
         nc.sync.dma_start(offsets[:], offs)
-        nc.scalar.dma_start(kc_sb[:, 0 : T // 2], kc[:, 0 : T // 2])
+        nc.scalar.dma_start(kc_sb[:, 0 : AHEAD * P], kc[:, 0 : AHEAD * P])
         nc.sync.dma_start(q_sb[:, 0:BANK], q[:, 0:BANK])
         nc.scalar.dma_start(q_sb[:, BANK:N], q[:, BANK:N])
         nc.sync.dma_start(mask_sb[0][:], mask[0:P, :])
+        nc.sync.dma_start(kc_sb[:, AHEAD * P : T], kc[:, AHEAD * P : T])
         nc.sync.dma_start(vc_ones[:, :, 0:D], vc.rearrange("(b p) d -> p b d", p=P))
-        nc.sync.dma_start(kc_sb[:, T // 2 : T], kc[:, T // 2 : T])
         for b in range(1, KEY_BLOCKS):
             nc.sync.dma_start(mask_sb[b][:], mask[b * P : (b + 1) * P, :])
         identity = held.tile([P, P], F32, name="identity")

@@ -18,7 +18,7 @@ BANK = 512
 PAIR = 2
 CUT = PAIR * P
 CUTS = N // CUT
-PITCH = 144
+PITCH = 160
 AHEAD = 2
 LATE = 2
 FLOPS = 4 * D * T * N
@@ -83,9 +83,9 @@ def tile_sdpasimple_kernel(tc, mask, q, kc, vc, offs, out):
             for c in range(lo // P, hi // P):
                 cut, i = divmod(c, PAIR)
                 nc.tensor.matmul(
-                    products[cut][:, i, 0 : D + 1],
+                    products[cut][:, i, :],
                     e_sb[:, c * P : (c + 1) * P],
-                    vc_ones[:, b, 0 : D + 1],
+                    vc_ones[:, b, :],
                     start=False,
                     stop=(b == KEY_BLOCKS - 1 and i == PAIR - 1),
                 )

import math

import concourse.mybir as mybir
from concourse.masks import make_identity

F32 = mybir.dt.float32
BF16 = mybir.dt.bfloat16
U16 = mybir.dt.uint16
ADD = mybir.AluOpType.add
COPY = mybir.ActivationFunctionType.Copy
EXP = mybir.ActivationFunctionType.Exp

P = 128
D, T, S, N = 128, 1024, 1024, 1024
SCALE = 1.0 / math.sqrt(D)
KEY_BLOCKS = T // P
BANK = 512
PAIR = 2
CUT = PAIR * P
CUTS = N // CUT
PITCH = 160
AHEAD = 2
LATE = 2
FLOPS = 4 * D * T * N


def tile_sdpasimple_kernel(tc, mask, q, kc, vc, offs, out):
    nc = tc.nc
    with (
        tc.tile_pool(name="held", bufs=1) as held,
        tc.tile_pool(name="work", bufs=4) as work,
        tc.tile_pool(name="small", bufs=8) as small,
        tc.psum_pool(name="product_banks", bufs=1) as product_banks,
        tc.psum_pool(name="other_banks", bufs=4) as other_banks,
    ):
        offsets = held.tile([P, N // 16], U16, name="offsets")
        kc_sb = held.tile([D, T], BF16, name="kc_sb")
        q_sb = held.tile([D, N], BF16, name="q_sb")
        mask_sb = [held.tile([P, S], F32, name=f"mask{b}") for b in range(KEY_BLOCKS)]
        vc_ones = held.tile([P, KEY_BLOCKS, PITCH], BF16, name="vc_ones")
        nc.gpsimd.memset(vc_ones[:, :, D:PITCH], 1.0)
        zeros = held.tile([P, P], BF16, name="zeros")
        nc.gpsimd.memset(zeros[:], 0.0)
        nc.sync.dma_start(offsets[:], offs)
        nc.scalar.dma_start(kc_sb[:, 0 : AHEAD * P], kc[:, 0 : AHEAD * P])
        nc.sync.dma_start(q_sb[:, 0:BANK], q[:, 0:BANK])
        nc.scalar.dma_start(q_sb[:, BANK:N], q[:, BANK:N])
        nc.sync.dma_start(mask_sb[0][:], mask[0:P, :])
        nc.sync.dma_start(kc_sb[:, AHEAD * P : T], kc[:, AHEAD * P : T])
        nc.sync.dma_start(vc_ones[:, :, 0:D], vc.rearrange("(b p) d -> p b d", p=P))
        for b in range(1, KEY_BLOCKS):
            nc.sync.dma_start(mask_sb[b][:], mask[b * P : (b + 1) * P, :])
        identity = held.tile([P, P], F32, name="identity")
        make_identity(nc, identity[:])

        scaled = {}
        products = []
        inverses = {}
        turned = {}

        def scores(b):
            scaled_sb = work.tile([P, N], F32, name="scaled_sb")
            for lo in range(0, N, BANK):
                score_ps = other_banks.tile([P, BANK], F32, name="score_ps", tag="bank")
                nc.tensor.matmul(
                    score_ps[:],
                    kc_sb[:, b * P : (b + 1) * P],
                    q_sb[:, lo : lo + BANK],
                    start=True,
                    stop=True,
                )
                nc.scalar.activation(scaled_sb[:, lo : lo + BANK], score_ps[:], COPY, scale=SCALE)
            scaled[b] = scaled_sb

        def weights(b, w_sb, e_sb, lo, hi):
            nc.vector.tensor_tensor(
                w_sb[:, lo:hi],
                mask_sb[b][:].indirect(offsets[:, lo // 16 : hi // 16]),
                scaled[b][:, lo:hi],
                ADD,
            )
            nc.scalar.activation(e_sb[:, lo:hi], w_sb[:, lo:hi], EXP)
            for c in range(lo // P, hi // P):
                cut, i = divmod(c, PAIR)
                nc.tensor.matmul(
                    products[cut][:, i, :],
                    e_sb[:, c * P : (c + 1) * P],
                    vc_ones[:, b, :],
                    start=False,
                    stop=(b == KEY_BLOCKS - 1 and i == PAIR - 1),
                )

        def divide(cut):
            inverse = small.tile([P, PAIR, 1], F32, name="inverse")
            nc.vector.reciprocal(inverse[:], products[cut][:, :, D : D + 1])
            out_ps = other_banks.tile([D, CUT], F32, name="out_ps", tag="bank")
            for i in range(PAIR):
                normal = small.tile([P, D], F32, name="normal")
                nc.scalar.activation(
                    normal[:], products[cut][:, i, 0:D], COPY, scale=inverse[:, i, :]
                )
                nc.tensor.transpose(out_ps[:, i * P : (i + 1) * P], normal[:], identity[:])
            turned[cut] = out_ps

        def leave(cut):
            out_sb = small.tile([D, CUT], F32, name="out_sb")
            nc.vector.tensor_copy(out_sb[:], turned[cut][:])
            nc.sync.dma_start(out[:, cut * CUT : (cut + 1) * CUT], out_sb[:])

        for b in range(AHEAD):
            scores(b)
        for cut in range(CUTS):
            product = product_banks.tile([P, PAIR, PITCH], F32, name=f"product{cut}")
            nc.tensor.matmul(product[:], zeros[:], q_sb[:, 0 : PAIR * PITCH], start=True, stop=False)
            products.append(product)
        for b in range(KEY_BLOCKS):
            if b + AHEAD < KEY_BLOCKS:
                scores(b + AHEAD)
            w_sb = work.tile([P, N], F32, name="w_sb")
            e_sb = work.tile([P, N], BF16, name="e_sb")
            if b == 0:
                for lo in range(0, N, BANK):
                    weights(b, w_sb, e_sb, lo, lo + BANK)
            elif b < KEY_BLOCKS - 1:
                weights(b, w_sb, e_sb, 0, N)
            else:
                for cut in range(CUTS + LATE):
                    if cut < CUTS:
                        weights(b, w_sb, e_sb, cut * CUT, (cut + 1) * CUT)
                    if cut >= LATE:
                        divide(cut - LATE)
        for cut in range(CUTS):
            leave(cut)
